import numpy as np
import ml_dtypes


def mxq(x, axis, fmt="e4m3"):
    dtype, down = {"e4m3": (ml_dtypes.float8_e4m3fn, 7), "e5m2": (ml_dtypes.float8_e5m2, 14)}[fmt]
    v = np.moveaxis(np.asarray(x, np.float32).astype(ml_dtypes.bfloat16).astype(np.float64), axis, -1)
    blocks = v.reshape(v.shape[:-1] + (-1, 32))
    amax = np.abs(blocks).max(-1, keepdims=True)
    byte = np.maximum(np.where(amax > 0, np.frexp(amax)[1] - 1 + 127, 0) - down, 1)
    scale = np.exp2(byte - 127.0)
    codes = (blocks / scale).astype(np.float32).astype(dtype).astype(np.float64)
    return np.moveaxis((codes * scale).reshape(v.shape), -1, axis)


WIDE = False


def mx_kscale(k):
    if not WIDE:
        return np.ones(k)
    levels = np.array([10, -10, 5, -5, 0])
    a = np.random.permutation(np.resize(levels, k // 512 * 4)).reshape(k // 512, 4)
    idx = np.arange(k)
    return np.exp2(a[idx // 512, idx % 128 // 32])


BF16 = ml_dtypes.bfloat16


def bf(x):
    return np.asarray(x, np.float32).astype(BF16)


def f64(x):
    return np.asarray(x).astype(np.float64)


E2M1 = np.array([0.0, 0.5, 1.0, 1.5, 2.0, 3.0, 4.0, 6.0, -0.0, -0.5, -1.0, -1.5, -2.0, -3.0, -4.0, -6.0])


def pack_weight(w, fmt):
    k, n = w.shape
    w = f64(bf(w)).reshape(k // 32, 32, n)
    amax = np.abs(w).max(1)
    if fmt == "e4m3":
        byte = np.frexp(amax)[1] - 1 + 127 - 7
    else:
        mant, ex = np.frexp(amax / 6.0)
        byte = np.where(mant > 0.5, ex, ex - 1) + 127
    byte = np.clip(np.where(amax > 0, byte, 1), 1, 254)
    scaled = (w * np.exp2(127.0 - byte)[:, None, :]).reshape(k, n).astype(np.float32)
    by_word = np.ascontiguousarray(scaled.reshape(k // 512, 128, 4, n).transpose(0, 1, 3, 2))
    if fmt == "e4m3":
        words = by_word.astype(ml_dtypes.float8_e4m3fn).view(np.uint8)
    else:
        c = by_word.astype(ml_dtypes.float4_e2m1fn).view(np.uint8) & 0xF
        words = c[..., 0::2] | (c[..., 1::2] << 4)
    return np.ascontiguousarray(words), np.ascontiguousarray(byte.astype(np.uint8).reshape(k // 512, 16, n))


def unpack_weight(words, scales, fmt):
    g, p, n, _ = words.shape
    if fmt == "e4m3":
        vals = np.ascontiguousarray(words).view(ml_dtypes.float8_e4m3fn).astype(np.float64)
    else:
        nib = np.empty((g, p, n, 4), np.uint8)
        nib[..., 0::2] = words & 0xF
        nib[..., 1::2] = words >> 4
        vals = E2M1[nib]
    vals = vals * np.repeat(np.exp2(scales.astype(np.float64) - 127.0), 8, axis=1)[..., None]
    return vals.transpose(0, 1, 3, 2).reshape(g * 512, n)

def pack4(w):
    words, scales = pack_weight(w, "e2m1")
    return words.reshape(words.shape[0], 128, -1), scales


def unpack4(words, scales):
    return unpack_weight(words.reshape(words.shape[0], 128, -1, 2), scales, "e2m1")


B, N, C, H = 2, 128, 2048, 16
EPS = 1e-6


def rmsnorm(v, w):
    var = np.mean(np.square(v), axis=-1, keepdims=True)
    return v * (1.0 / np.sqrt(var + EPS)) * w


def setup_inputs():
    s = mx_kscale(C)
    x = bf(np.random.standard_normal((B, N, C)) * s)
    w = np.random.standard_normal((3 * C, C)) / np.sqrt(C) / s[None, :]
    words, scales = pack4(np.ascontiguousarray(w.T))
    q_norm_w = bf(1.0 + 0.1 * np.random.standard_normal(C))
    k_norm_w = bf(1.0 + 0.1 * np.random.standard_normal(C))
    return {"x": x,
            "w_qkv_words": words,
            "w_qkv_scales": scales,
            "q_norm_w": q_norm_w,
            "k_norm_w": k_norm_w}


def reference(x, w_qkv_words, w_qkv_scales, q_norm_w, k_norm_w):
    xq = mxq(f64(x), 2, "e4m3")
    wt = unpack4(w_qkv_words, w_qkv_scales)
    q = xq @ wt[:, :C]
    k = xq @ wt[:, C:2 * C]
    v = xq @ wt[:, 2 * C:]
    return rmsnorm(q, f64(q_norm_w)), rmsnorm(k, f64(k_norm_w)), v

@@ -1,0 +1,166 @@
+from contextlib import ExitStack
+
+import concourse.mybir as mybir
+from concourse.masks import make_identity
+
+F32 = mybir.dt.float32
+BF16 = mybir.dt.bfloat16
+I32 = mybir.dt.int32
+U32 = mybir.dt.uint32
+U8 = mybir.dt.uint8
+FP8X4 = mybir.dt.float8_e4m3fn_x4
+FP4X4 = mybir.dt.float4_e2m1fn_x4
+ACT = mybir.ActivationFunctionType
+ALU = mybir.AluOpType
+
+P = 128
+TOKEN_TILES = 2
+C = 2048
+K_PASS = 512
+GROUPS = C // K_PASS
+N_TILE = 512
+CHUNKS = C // N_TILE
+PARTS = 3
+NORMED_PARTS = 2
+EPS = 1e-6
+
+FLOPS = 2 * TOKEN_TILES * P * C * PARTS * C
+
+
+def load_scale_rows(nc, plane, w_qkv_scales, part):
+    cols = slice(part * C, (part + 1) * C)
+    for g in range(0, GROUPS, 2):
+        for j in range(8):
+            partition = 32 * (j // 4) + j % 4
+            nc.sync.dma_start(
+                out=plane[partition:P:64, g : g + 2, :].bitcast(I32),
+                in_=w_qkv_scales[g : g + 2, j:16:8, cols].rearrange("g j n -> j g n").bitcast(I32),
+            )
+
+
+def tile_internattention_pa_kernel(
+    tc, x, w_qkv_words, w_qkv_scales, q_norm_w, k_norm_w, out_0, out_1, out_2
+):
+    nc = tc.nc
+    outs = (out_0, out_1, out_2)
+    with ExitStack() as stack:
+        stack.enter_context(tc.manual_schedule())
+        keep = stack.enter_context(tc.tile_pool(name="keep", bufs=1))
+        rows = stack.enter_context(tc.tile_pool(name="rows", bufs=4))
+        scratch = stack.enter_context(tc.tile_pool(name="scratch", bufs=4))
+        stats = stack.enter_context(tc.tile_pool(name="stats", bufs=4))
+        psum = stack.enter_context(tc.psum_pool(name="psum", bufs=8))
+
+        ident_bf = keep.tile([P, P], BF16)
+        make_identity(nc, ident_bf[:])
+        ident_f32 = keep.tile([P, P], F32)
+        make_identity(nc, ident_f32[:])
+
+        gain_rows = keep.tile([P, N_TILE], BF16)
+        nc.vector.memset(gain_rows[:], 0.0)
+        nc.scalar.dma_start(out=gain_rows[0:CHUNKS, :], in_=q_norm_w.rearrange("(c n) -> c n", n=N_TILE))
+        nc.scalar.dma_start(out=gain_rows[CHUNKS : 2 * CHUNKS, :], in_=k_norm_w.rearrange("(c n) -> c n", n=N_TILE))
+
+        eps = keep.tile([P, 1], F32)
+        nc.vector.memset(eps[:], EPS)
+        table_warm = keep.tile([P, 1], F32)
+        nc.scalar.activation(out=table_warm[:], in_=eps[:], func=ACT.Sqrt)
+
+        x_sb = keep.tile([P, TOKEN_TILES, C], BF16)
+        nc.sync.dma_start(out=x_sb[:], in_=x.rearrange("b p k -> p b k"))
+
+        w_words = []
+        w_planes = []
+        for part in range(PARTS):
+            words = keep.tile([P, GROUPS, 2 * C], U8, name="w_words%d" % part, align_bytes=64)
+            plane = keep.tile([P, GROUPS, C], U8, name="w_plane%d" % part, align_bytes=64)
+            nc.vector.memset(plane[:].bitcast(I32), 0)
+            load_scale_rows(nc, plane, w_qkv_scales, part)
+            for g in range(GROUPS):
+                nc.sync.dma_start(
+                    out=words[:, g, :].bitcast(I32),
+                    in_=w_qkv_words[g, :, part * 2 * C : (part + 1) * 2 * C].bitcast(I32),
+                )
+            w_words.append(words)
+            w_planes.append(plane)
+
+        gain_all = keep.tile([P, NORMED_PARTS, C], BF16)
+        for part in range(NORMED_PARTS):
+            for half in range(2):
+                gain_ps = psum.tile([P, 2 * N_TILE], BF16, name="gain_ps", tag="bank")
+                for i in range(2):
+                    r = part * CHUNKS + 2 * half + i
+                    nc.tensor.matmul(
+                        out=gain_ps[:, i * N_TILE : (i + 1) * N_TILE],
+                        lhsT=ident_bf[:, r : r + 1].to_broadcast([P, P]),
+                        rhs=gain_rows[:],
+                        start=True,
+                        stop=True,
+                    )
+                nc.scalar.copy(out=gain_all[:, part, half * 2 * N_TILE : (half + 1) * 2 * N_TILE], in_=gain_ps[:])
+
+        x_pairs = x_sb[:].bitcast(F32)
+        grouped = keep.tile([P, GROUPS, TOKEN_TILES * P * 4], BF16, align_bytes=64)
+        x_codes = keep.tile([P, GROUPS, TOKEN_TILES * P], U32, align_bytes=64)
+        x_scales = keep.tile([P, GROUPS, TOKEN_TILES * P], U8, align_bytes=64)
+        for g in range(GROUPS):
+            xt = psum.tile([P, TOKEN_TILES, 2, P], F32, name="xt", tag="bank")
+            for tile in range(TOKEN_TILES):
+                for u in range(2):
+                    nc.tensor.transpose(
+                        xt[:, tile, u, :],
+                        x_pairs[:, tile, (K_PASS // 2) * g + u : (K_PASS // 2) * (g + 1) : 2],
+                        ident_f32[:],
+                    )
+            nc.vector.tensor_copy(
+                out=grouped[:, g, :].bitcast(F32).rearrange("p (a r u) -> p a r u", a=TOKEN_TILES, u=2),
+                in_=xt[:].rearrange("p a u r -> p a r u"),
+            )
+            nc.vector.quantize_mx(
+                out=x_codes[:, g, :].bitcast(FP8X4), scales=x_scales[:, g, :], in_=grouped[:, g, :]
+            )
+
+        for part in range(PARTS):
+            for tile in range(TOKEN_TILES):
+                tokens = slice(tile * P, (tile + 1) * P)
+                acc = [psum.tile([P, N_TILE], F32, name="acc%d" % c, tag="bank") for c in range(CHUNKS)]
+                for g in range(GROUPS):
+                    for c in range(CHUNKS):
+                        nc.tensor.matmul_mx(
+                            out=acc[c][:],
+                            lhsT=x_codes[:, g, tokens].bitcast(FP8X4),
+                            lhsT_scale=x_scales[:, g, tokens],
+                            rhs=w_words[part][:, g, c * 2 * N_TILE : (c + 1) * 2 * N_TILE].bitcast(FP4X4),
+                            rhs_scale=w_planes[part][:, g, c * N_TILE : (c + 1) * N_TILE],
+                            start=(g == 0),
+                            stop=(g == GROUPS - 1),
+                        )
+
+                y = rows.tile([P, C], F32, name="y")
+                if part < NORMED_PARTS:
+                    sum_sq = stats.tile([P, CHUNKS], F32, name="sum_sq")
+                    for c in range(CHUNKS):
+                        cols = slice(c * N_TILE, (c + 1) * N_TILE)
+                        squares = scratch.tile([P, N_TILE], BF16, name="squares")
+                        nc.scalar.activation(
+                            out=squares[:], in_=acc[c][:], func=ACT.Square, accum_out=sum_sq[:, c : c + 1]
+                        )
+                        nc.vector.tensor_tensor(
+                            out=y[:, cols], in0=acc[c][:], in1=gain_all[:, part, cols], op=ALU.mult
+                        )
+                    total = stats.tile([P, 1], F32, name="total")
+                    nc.vector.tensor_reduce(out=total[:], in_=sum_sq[:], axis=mybir.AxisListType.X, op=ALU.add)
+                    rms = stats.tile([P, 1], F32, name="rms")
+                    nc.scalar.activation(out=rms[:], in_=total[:], func=ACT.Sqrt, scale=1.0 / C, bias=eps[:, 0:1])
+                    inv_rms = stats.tile([P, 1], F32, name="inv_rms")
+                    nc.vector.reciprocal(out=inv_rms[:], in_=rms[:])
+                    nc.vector.tensor_scalar_mul(out=y[:], in0=y[:], scalar1=inv_rms[:, 0:1])
+                    nc.sync.dma_start(out=outs[part][tile], in_=y[:])
+                else:
+                    for c in range(CHUNKS):
+                        cols = slice(c * N_TILE, (c + 1) * N_TILE)
+                        if c % 2 == 0:
+                            nc.scalar.copy(out=y[:, cols], in_=acc[c][:])
+                        else:
+                            nc.vector.tensor_copy(out=y[:, cols], in_=acc[c][:])
+                        nc.sync.dma_start(out=outs[part][tile][:, cols], in_=y[:, cols])

@@ -20,6 +20,7 @@ K_PASS = 512
 GROUPS = C // K_PASS
 N_TILE = 512
 CHUNKS = C // N_TILE
+N_NARROW = 128
 PARTS = 3
 NORMED_PARTS = 2
 EPS = 1e-6
@@ -29,13 +30,12 @@ FLOPS = 2 * TOKEN_TILES * P * C * PARTS * C
 
 def load_scale_rows(nc, plane, w_qkv_scales, part):
     cols = slice(part * C, (part + 1) * C)
-    for g in range(0, GROUPS, 2):
-        for j in range(8):
-            partition = 32 * (j // 4) + j % 4
-            nc.sync.dma_start(
-                out=plane[partition:P:64, g : g + 2, :].bitcast(I32),
-                in_=w_qkv_scales[g : g + 2, j:16:8, cols].rearrange("g j n -> j g n").bitcast(I32),
-            )
+    for j in range(8):
+        partition = 32 * (j // 4) + j % 4
+        nc.sync.dma_start(
+            out=plane[partition:P:64, :, :].bitcast(I32),
+            in_=w_qkv_scales[:, j:16:8, cols].rearrange("g j n -> j g n").bitcast(I32),
+        )
 
 
 def tile_internattention_pa_kernel(
@@ -76,10 +76,13 @@ def tile_internattention_pa_kernel(
             plane = keep.tile([P, GROUPS, C], U8, name="w_plane%d" % part, align_bytes=64)
             nc.vector.memset(plane[:].bitcast(I32), 0)
             load_scale_rows(nc, plane, w_qkv_scales, part)
-            for g in range(GROUPS):
+            pieces = [(0, 1), (1, 2), (2, 3), (3, 4)] if part == 0 else [(0, 1), (1, 2), (2, 4)]
+            for g0, g1 in pieces:
                 nc.sync.dma_start(
-                    out=words[:, g, :].bitcast(I32),
-                    in_=w_qkv_words[g, :, part * 2 * C : (part + 1) * 2 * C].bitcast(I32),
+                    out=words[:, g0:g1, :].bitcast(I32),
+                    in_=w_qkv_words[g0:g1, :, part * 2 * C : (part + 1) * 2 * C]
+                    .rearrange("g p n -> p g n")
+                    .bitcast(I32),
                 )
             w_words.append(words)
             w_planes.append(plane)
@@ -123,18 +126,26 @@ def tile_internattention_pa_kernel(
         for part in range(PARTS):
             for tile in range(TOKEN_TILES):
                 tokens = slice(tile * P, (tile + 1) * P)
-                acc = [psum.tile([P, N_TILE], F32, name="acc%d" % c, tag="bank") for c in range(CHUNKS)]
-                for g in range(GROUPS):
-                    for c in range(CHUNKS):
-                        nc.tensor.matmul_mx(
-                            out=acc[c][:],
-                            lhsT=x_codes[:, g, tokens].bitcast(FP8X4),
-                            lhsT_scale=x_scales[:, g, tokens],
-                            rhs=w_words[part][:, g, c * 2 * N_TILE : (c + 1) * 2 * N_TILE].bitcast(FP4X4),
-                            rhs_scale=w_planes[part][:, g, c * N_TILE : (c + 1) * N_TILE],
-                            start=(g == 0),
-                            stop=(g == GROUPS - 1),
-                        )
+                last_unit = part == PARTS - 1 and tile == TOKEN_TILES - 1
+                banks = [(c * N_TILE, N_TILE) for c in range(CHUNKS)]
+                if last_unit:
+                    banks = banks[:-1] + [(C - N_TILE + i * N_NARROW, N_NARROW) for i in range(N_TILE // N_NARROW)]
+                acc = [psum.tile([P, width], F32, name="acc", tag="bank") for col0, width in banks]
+                if last_unit:
+                    passes = [(g, b) for b in range(len(banks)) for g in range(GROUPS)]
+                else:
+                    passes = [(g, b) for g in range(GROUPS) for b in range(len(banks))]
+                for g, b in passes:
+                    col0, width = banks[b]
+                    nc.tensor.matmul_mx(
+                        out=acc[b][:],
+                        lhsT=x_codes[:, g, tokens].bitcast(FP8X4),
+                        lhsT_scale=x_scales[:, g, tokens],
+                        rhs=w_words[part][:, g, 2 * col0 : 2 * (col0 + width)].bitcast(FP4X4),
+                        rhs_scale=w_planes[part][:, g, col0 : col0 + width],
+                        start=(g == 0),
+                        stop=(g == GROUPS - 1),
+                    )
 
                 y = rows.tile([P, C], F32, name="y")
                 if part < NORMED_PARTS:
@@ -157,10 +168,14 @@ def tile_internattention_pa_kernel(
                     nc.vector.tensor_scalar_mul(out=y[:], in0=y[:], scalar1=inv_rms[:, 0:1])
                     nc.sync.dma_start(out=outs[part][tile], in_=y[:])
                 else:
-                    for c in range(CHUNKS):
-                        cols = slice(c * N_TILE, (c + 1) * N_TILE)
-                        if c % 2 == 0:
-                            nc.scalar.copy(out=y[:, cols], in_=acc[c][:])
+                    stored = 0
+                    for b, (col0, width) in enumerate(banks):
+                        if b % 2 == 0:
+                            nc.scalar.copy(out=y[:, col0 : col0 + width], in_=acc[b][:])
                         else:
-                            nc.vector.tensor_copy(out=y[:, cols], in_=acc[c][:])
-                        nc.sync.dma_start(out=outs[part][tile][:, cols], in_=y[:, cols])
+                            nc.vector.tensor_copy(out=y[:, col0 : col0 + width], in_=acc[b][:])
+                        if (b >= 1) if last_unit else (b == len(banks) - 1):
+                            nc.sync.dma_start(
+                                out=outs[part][tile][:, stored : col0 + width], in_=y[:, stored : col0 + width]
+                            )
+                            stored = col0 + width

from contextlib import ExitStack

import concourse.mybir as mybir
from concourse.masks import make_identity

F32 = mybir.dt.float32
BF16 = mybir.dt.bfloat16
I32 = mybir.dt.int32
U32 = mybir.dt.uint32
U8 = mybir.dt.uint8
FP8X4 = mybir.dt.float8_e4m3fn_x4
FP4X4 = mybir.dt.float4_e2m1fn_x4
ACT = mybir.ActivationFunctionType
ALU = mybir.AluOpType

P = 128
TOKEN_TILES = 2
C = 2048
K_PASS = 512
GROUPS = C // K_PASS
N_TILE = 512
CHUNKS = C // N_TILE
N_NARROW = 128
PARTS = 3
NORMED_PARTS = 2
EPS = 1e-6

FLOPS = 2 * TOKEN_TILES * P * C * PARTS * C


def load_scale_rows(nc, plane, w_qkv_scales, part):
    cols = slice(part * C, (part + 1) * C)
    for j in range(8):
        partition = 32 * (j // 4) + j % 4
        nc.sync.dma_start(
            out=plane[partition:P:64, :, :].bitcast(I32),
            in_=w_qkv_scales[:, j:16:8, cols].rearrange("g j n -> j g n").bitcast(I32),
        )


def tile_internattention_pa_kernel(
    tc, x, w_qkv_words, w_qkv_scales, q_norm_w, k_norm_w, out_0, out_1, out_2
):
    nc = tc.nc
    outs = (out_0, out_1, out_2)
    with ExitStack() as stack:
        stack.enter_context(tc.manual_schedule())
        keep = stack.enter_context(tc.tile_pool(name="keep", bufs=1))
        rows = stack.enter_context(tc.tile_pool(name="rows", bufs=4))
        scratch = stack.enter_context(tc.tile_pool(name="scratch", bufs=4))
        stats = stack.enter_context(tc.tile_pool(name="stats", bufs=4))
        psum = stack.enter_context(tc.psum_pool(name="psum", bufs=8))

        ident_bf = keep.tile([P, P], BF16)
        make_identity(nc, ident_bf[:])
        ident_f32 = keep.tile([P, P], F32)
        make_identity(nc, ident_f32[:])

        gain_rows = keep.tile([P, N_TILE], BF16)
        nc.vector.memset(gain_rows[:], 0.0)
        nc.scalar.dma_start(out=gain_rows[0:CHUNKS, :], in_=q_norm_w.rearrange("(c n) -> c n", n=N_TILE))
        nc.scalar.dma_start(out=gain_rows[CHUNKS : 2 * CHUNKS, :], in_=k_norm_w.rearrange("(c n) -> c n", n=N_TILE))

        eps = keep.tile([P, 1], F32)
        nc.vector.memset(eps[:], EPS)
        table_warm = keep.tile([P, 1], F32)
        nc.scalar.activation(out=table_warm[:], in_=eps[:], func=ACT.Sqrt)

        x_sb = keep.tile([P, TOKEN_TILES, C], BF16)
        nc.sync.dma_start(out=x_sb[:], in_=x.rearrange("b p k -> p b k"))

        w_words = []
        w_planes = []
        for part in range(PARTS):
            words = keep.tile([P, GROUPS, 2 * C], U8, name="w_words%d" % part, align_bytes=64)
            plane = keep.tile([P, GROUPS, C], U8, name="w_plane%d" % part, align_bytes=64)
            nc.vector.memset(plane[:].bitcast(I32), 0)
            load_scale_rows(nc, plane, w_qkv_scales, part)
            pieces = [(0, 1), (1, 2), (2, 3), (3, 4)] if part == 0 else [(0, 1), (1, 2), (2, 4)]
            for g0, g1 in pieces:
                nc.sync.dma_start(
                    out=words[:, g0:g1, :].bitcast(I32),
                    in_=w_qkv_words[g0:g1, :, part * 2 * C : (part + 1) * 2 * C]
                    .rearrange("g p n -> p g n")
                    .bitcast(I32),
                )
            w_words.append(words)
            w_planes.append(plane)

        gain_all = keep.tile([P, NORMED_PARTS, C], BF16)
        for part in range(NORMED_PARTS):
            for half in range(2):
                gain_ps = psum.tile([P, 2 * N_TILE], BF16, name="gain_ps", tag="bank")
                for i in range(2):
                    r = part * CHUNKS + 2 * half + i
                    nc.tensor.matmul(
                        out=gain_ps[:, i * N_TILE : (i + 1) * N_TILE],
                        lhsT=ident_bf[:, r : r + 1].to_broadcast([P, P]),
                        rhs=gain_rows[:],
                        start=True,
                        stop=True,
                    )
                nc.scalar.copy(out=gain_all[:, part, half * 2 * N_TILE : (half + 1) * 2 * N_TILE], in_=gain_ps[:])

        x_pairs = x_sb[:].bitcast(F32)
        grouped = keep.tile([P, GROUPS, TOKEN_TILES * P * 4], BF16, align_bytes=64)
        x_codes = keep.tile([P, GROUPS, TOKEN_TILES * P], U32, align_bytes=64)
        x_scales = keep.tile([P, GROUPS, TOKEN_TILES * P], U8, align_bytes=64)
        for g in range(GROUPS):
            xt = psum.tile([P, TOKEN_TILES, 2, P], F32, name="xt", tag="bank")
            for tile in range(TOKEN_TILES):
                for u in range(2):
                    nc.tensor.transpose(
                        xt[:, tile, u, :],
                        x_pairs[:, tile, (K_PASS // 2) * g + u : (K_PASS // 2) * (g + 1) : 2],
                        ident_f32[:],
                    )
            nc.vector.tensor_copy(
                out=grouped[:, g, :].bitcast(F32).rearrange("p (a r u) -> p a r u", a=TOKEN_TILES, u=2),
                in_=xt[:].rearrange("p a u r -> p a r u"),
            )
            nc.vector.quantize_mx(
                out=x_codes[:, g, :].bitcast(FP8X4), scales=x_scales[:, g, :], in_=grouped[:, g, :]
            )

        for part in range(PARTS):
            for tile in range(TOKEN_TILES):
                tokens = slice(tile * P, (tile + 1) * P)
                last_unit = part == PARTS - 1 and tile == TOKEN_TILES - 1
                banks = [(c * N_TILE, N_TILE) for c in range(CHUNKS)]
                if last_unit:
                    banks = banks[:-1] + [(C - N_TILE + i * N_NARROW, N_NARROW) for i in range(N_TILE // N_NARROW)]
                acc = [psum.tile([P, width], F32, name="acc", tag="bank") for col0, width in banks]
                if last_unit:
                    passes = [(g, b) for b in range(len(banks)) for g in range(GROUPS)]
                else:
                    passes = [(g, b) for g in range(GROUPS) for b in range(len(banks))]
                for g, b in passes:
                    col0, width = banks[b]
                    nc.tensor.matmul_mx(
                        out=acc[b][:],
                        lhsT=x_codes[:, g, tokens].bitcast(FP8X4),
                        lhsT_scale=x_scales[:, g, tokens],
                        rhs=w_words[part][:, g, 2 * col0 : 2 * (col0 + width)].bitcast(FP4X4),
                        rhs_scale=w_planes[part][:, g, col0 : col0 + width],
                        start=(g == 0),
                        stop=(g == GROUPS - 1),
                    )

                y = rows.tile([P, C], F32, name="y")
                if part < NORMED_PARTS:
                    sum_sq = stats.tile([P, CHUNKS], F32, name="sum_sq")
                    for c in range(CHUNKS):
                        cols = slice(c * N_TILE, (c + 1) * N_TILE)
                        squares = scratch.tile([P, N_TILE], BF16, name="squares")
                        nc.scalar.activation(
                            out=squares[:], in_=acc[c][:], func=ACT.Square, accum_out=sum_sq[:, c : c + 1]
                        )
                        nc.vector.tensor_tensor(
                            out=y[:, cols], in0=acc[c][:], in1=gain_all[:, part, cols], op=ALU.mult
                        )
                    total = stats.tile([P, 1], F32, name="total")
                    nc.vector.tensor_reduce(out=total[:], in_=sum_sq[:], axis=mybir.AxisListType.X, op=ALU.add)
                    rms = stats.tile([P, 1], F32, name="rms")
                    nc.scalar.activation(out=rms[:], in_=total[:], func=ACT.Sqrt, scale=1.0 / C, bias=eps[:, 0:1])
                    inv_rms = stats.tile([P, 1], F32, name="inv_rms")
                    nc.vector.reciprocal(out=inv_rms[:], in_=rms[:])
                    nc.vector.tensor_scalar_mul(out=y[:], in0=y[:], scalar1=inv_rms[:, 0:1])
                    nc.sync.dma_start(out=outs[part][tile], in_=y[:])
                else:
                    stored = 0
                    for b, (col0, width) in enumerate(banks):
                        if b % 2 == 0:
                            nc.scalar.copy(out=y[:, col0 : col0 + width], in_=acc[b][:])
                        else:
                            nc.vector.tensor_copy(out=y[:, col0 : col0 + width], in_=acc[b][:])
                        if (b >= 1) if last_unit else (b == len(banks) - 1):
                            nc.sync.dma_start(
                                out=outs[part][tile][:, stored : col0 + width], in_=y[:, stored : col0 + width]
                            )
                            stored = col0 + width
